import numpy as np
import ml_dtypes

BF16 = ml_dtypes.bfloat16


def bf(x):
    return np.asarray(x, np.float32).astype(BF16)


def f32(x):
    return np.asarray(x, np.float32)


def f64(x):
    return np.asarray(x).astype(np.float64)


def striped(idx):
    return np.tile(idx.reshape(-1, 16).T, (8, 1))


EMB, ENC, H, NG, S, N = 128, 512, 512, 4, 1024, 512


def sigmoid(v):
    return 1.0 / (1.0 + np.exp(-v))


def setup_inputs():
    sc = 1.0 / np.sqrt(EMB + ENC + H)
    return {
        "base": f32(0.3 * np.random.standard_normal((H, S))),
        "x": bf(np.random.standard_normal((EMB + ENC, N))),
        "h0": bf(np.random.standard_normal((H, N))),
        "c0": f32(np.random.standard_normal((H, N))),
        "W_ih": bf(sc * np.random.standard_normal((EMB + ENC, NG * H))),
        "W_hh": bf(sc * np.random.standard_normal((H, NG * H))),
        "b_ih": f32(0.2 * np.random.standard_normal((NG * H, 1))),
        "b_hh": f32(0.2 * np.random.standard_normal((NG * H, 1))),
        "offs": striped(np.random.permutation(S)[:N]),
    }


def reference(base, x, h0, c0, W_ih, W_hh, b_ih, b_hh, offs):
    idx = offs[:16].T.reshape(-1)
    pre = f64(W_ih).T @ f64(x) + f64(W_hh).T @ f64(h0) + f64(b_ih) + f64(b_hh)
    p_i, p_f, p_u, p_o = np.split(pre, NG, axis=0)
    cnew = sigmoid(p_f) * f64(c0) + sigmoid(p_i) * np.tanh(p_u)
    res = f64(base).copy()
    res[:, idx] = sigmoid(p_o) * np.tanh(cnew)
    return res

@@ -1,0 +1,86 @@
+import concourse.mybir as mybir
+from concourse.masks import make_identity
+
+BF16, F32, U16 = mybir.dt.bfloat16, mybir.dt.float32, mybir.dt.uint16
+SIGMOID = mybir.ActivationFunctionType.Sigmoid
+TANH = mybir.ActivationFunctionType.Tanh
+MULT = mybir.AluOpType.mult
+
+P = 128
+IN, H, GATES, SLOTS, N = 640, 512, 4, 1024, 512
+K_TILES_X, K_TILES_H = IN // P, H // P
+K_TILES = K_TILES_X + K_TILES_H
+BLOCKS = H // P
+ROW_BLOCKS = GATES * BLOCKS
+GATE_I, GATE_F, GATE_U, GATE_O = 0, 1, 2, 3
+
+FLOPS = 2 * (IN + H) * GATES * H * N
+
+
+def tile_pgndecoder_s_kernel(tc, base, x, h0, c0, W_ih, W_hh, b_ih, b_hh, offs, out):
+    nc = tc.nc
+    with (
+        tc.tile_pool(name="held", bufs=1) as held,
+        tc.tile_pool(name="work", bufs=2) as work,
+        tc.psum_pool(name="psum", bufs=8) as psum,
+    ):
+        offsets = held.tile([P, N // 16], U16, name="offsets")
+        nc.sync.dma_start(offsets[:], offs)
+
+        bias_rows = held.tile([P, P], F32, name="bias_rows")
+        nc.vector.memset(bias_rows[:], 0.0)
+        nc.gpsimd.dma_start(bias_rows[0:ROW_BLOCKS, :], b_ih.rearrange("(m p) o -> m (p o)", p=P))
+        nc.gpsimd.dma_start(bias_rows[ROW_BLOCKS : 2 * ROW_BLOCKS, :], b_hh.rearrange("(m p) o -> m (p o)", p=P))
+        identity = held.tile([P, P], F32, name="identity")
+        make_identity(nc, identity[:])
+
+        sources = [(x, W_ih, t) for t in range(K_TILES_X)] + [(h0, W_hh, t) for t in range(K_TILES_H)]
+        acts, weights = [], []
+        for k, (act_dram, w_dram, t) in enumerate(sources):
+            act = held.tile([P, N], BF16, name=f"act{k}")
+            nc.scalar.dma_start(act[:], act_dram[t * P : (t + 1) * P, :])
+            acts.append(act)
+            w = held.tile([P, GATES * H], BF16, name=f"w{k}")
+            nc.sync.dma_start(w[:], w_dram[t * P : (t + 1) * P, :])
+            weights.append(w)
+
+        cells, windows = [], []
+        for b in range(BLOCKS):
+            cell = held.tile([P, N], F32, name=f"cell{b}")
+            nc.scalar.dma_start(cell[:], c0[b * P : (b + 1) * P, :])
+            cells.append(cell)
+            window = held.tile([P, SLOTS], F32, name=f"window{b}")
+            nc.scalar.dma_start(window[:], base[b * P : (b + 1) * P, :])
+            windows.append(window)
+
+        bias_t = psum.tile([P, P], F32, name="bias_t", tag="acc")
+        nc.tensor.transpose(bias_t[:], bias_rows[:], identity[:])
+        bias_cols = held.tile([P, 2 * ROW_BLOCKS], F32, name="bias_cols")
+        nc.vector.tensor_copy(bias_cols[:], bias_t[:, 0 : 2 * ROW_BLOCKS])
+        bias = held.tile([P, ROW_BLOCKS], F32, name="bias")
+        nc.vector.tensor_add(bias[:], bias_cols[:, 0:ROW_BLOCKS], bias_cols[:, ROW_BLOCKS : 2 * ROW_BLOCKS])
+
+        for b in range(BLOCKS):
+            gate = []
+            for g in range(GATES):
+                m = g * BLOCKS + b
+                acc = psum.tile([P, N], F32, name="acc")
+                for k in range(K_TILES):
+                    nc.tensor.matmul(
+                        acc[:], weights[k][:, m * P : (m + 1) * P], acts[k][:], start=(k == 0), stop=(k == K_TILES - 1)
+                    )
+                squashed = work.tile([P, N], F32, name=f"gate{g}")
+                nc.scalar.activation(squashed[:], acc[:], TANH if g == GATE_U else SIGMOID, bias=bias[:, m : m + 1])
+                gate.append(squashed)
+
+            kept = work.tile([P, N], F32, name="kept")
+            nc.vector.tensor_mul(kept[:], gate[GATE_F][:], cells[b][:])
+            fresh = work.tile([P, N], F32, name="fresh")
+            nc.vector.tensor_mul(fresh[:], gate[GATE_I][:], gate[GATE_U][:])
+            cnew = work.tile([P, N], F32, name="cnew")
+            nc.vector.tensor_add(cnew[:], kept[:], fresh[:])
+            tanh_c = work.tile([P, N], F32, name="tanh_c")
+            nc.scalar.activation(tanh_c[:], cnew[:], TANH)
+
+            nc.vector.tensor_tensor(windows[b][:].indirect(offsets[:]), gate[GATE_O][:], tanh_c[:], MULT)
+            nc.sync.dma_start(out[b * P : (b + 1) * P, :], windows[b][:])

@@ -1,5 +1,4 @@
 import concourse.mybir as mybir
-from concourse.masks import make_identity
 
 BF16, F32, U16 = mybir.dt.bfloat16, mybir.dt.float32, mybir.dt.uint16
 SIGMOID = mybir.ActivationFunctionType.Sigmoid
@@ -13,6 +12,8 @@ K_TILES = K_TILES_X + K_TILES_H
 BLOCKS = H // P
 ROW_BLOCKS = GATES * BLOCKS
 GATE_I, GATE_F, GATE_U, GATE_O = 0, 1, 2, 3
+PAIR = 2
+SQ = 32
 
 FLOPS = 2 * (IN + H) * GATES * H * N
 
@@ -22,57 +23,57 @@ def tile_pgndecoder_s_kernel(tc, base, x, h0, c0, W_ih, W_hh, b_ih, b_hh, offs, 
     with (
         tc.tile_pool(name="held", bufs=1) as held,
         tc.tile_pool(name="work", bufs=2) as work,
-        tc.psum_pool(name="psum", bufs=8) as psum,
+        tc.psum_pool(name="psum", bufs=GATES * PAIR) as psum,
     ):
         offsets = held.tile([P, N // 16], U16, name="offsets")
         nc.sync.dma_start(offsets[:], offs)
 
-        bias_rows = held.tile([P, P], F32, name="bias_rows")
-        nc.vector.memset(bias_rows[:], 0.0)
-        nc.gpsimd.dma_start(bias_rows[0:ROW_BLOCKS, :], b_ih.rearrange("(m p) o -> m (p o)", p=P))
-        nc.gpsimd.dma_start(bias_rows[ROW_BLOCKS : 2 * ROW_BLOCKS, :], b_hh.rearrange("(m p) o -> m (p o)", p=P))
-        identity = held.tile([P, P], F32, name="identity")
-        make_identity(nc, identity[:])
-
         sources = [(x, W_ih, t) for t in range(K_TILES_X)] + [(h0, W_hh, t) for t in range(K_TILES_H)]
-        acts, weights = [], []
+        acts = []
         for k, (act_dram, w_dram, t) in enumerate(sources):
             act = held.tile([P, N], BF16, name=f"act{k}")
             nc.scalar.dma_start(act[:], act_dram[t * P : (t + 1) * P, :])
             acts.append(act)
-            w = held.tile([P, GATES * H], BF16, name=f"w{k}")
-            nc.sync.dma_start(w[:], w_dram[t * P : (t + 1) * P, :])
-            weights.append(w)
+        w_half = [[], []]
+        for half in range(2):
+            for k, (act_dram, w_dram, t) in enumerate(sources):
+                w = held.tile([P, GATES, PAIR * P], BF16, name=f"w{half}_{k}")
+                by_gate = w_dram[t * P : (t + 1) * P, :].rearrange("p (g c) -> p g c", g=GATES)
+                nc.sync.dma_start(w[:], by_gate[:, :, half * PAIR * P : (half + 1) * PAIR * P])
+                w_half[half].append(w)
 
         cells, windows = [], []
         for b in range(BLOCKS):
             cell = held.tile([P, N], F32, name=f"cell{b}")
-            nc.scalar.dma_start(cell[:], c0[b * P : (b + 1) * P, :])
+            nc.sync.dma_start(cell[:], c0[b * P : (b + 1) * P, :])
             cells.append(cell)
             window = held.tile([P, SLOTS], F32, name=f"window{b}")
-            nc.scalar.dma_start(window[:], base[b * P : (b + 1) * P, :])
+            nc.sync.dma_start(window[:], base[b * P : (b + 1) * P, :])
             windows.append(window)
 
-        bias_t = psum.tile([P, P], F32, name="bias_t", tag="acc")
-        nc.tensor.transpose(bias_t[:], bias_rows[:], identity[:])
-        bias_cols = held.tile([P, 2 * ROW_BLOCKS], F32, name="bias_cols")
-        nc.vector.tensor_copy(bias_cols[:], bias_t[:, 0 : 2 * ROW_BLOCKS])
+        bias_in = held.tile([P, SQ], F32, name="bias_in", align_bytes=64)
+        for a in range(P // SQ):
+            for v, b_dram in enumerate((b_ih, b_hh)):
+                first = a * SQ + v * ROW_BLOCKS
+                runs = b_dram.rearrange("(m a i) o -> a m (i o)", a=P // SQ, i=SQ)
+                nc.scalar.dma_start(bias_in[first : first + ROW_BLOCKS, :], runs[a])
+        bias_t = held.tile([P, SQ], F32, name="bias_t", align_bytes=64)
+        nc.vector.transpose(bias_t[:], bias_in[:])
         bias = held.tile([P, ROW_BLOCKS], F32, name="bias")
-        nc.vector.tensor_add(bias[:], bias_cols[:, 0:ROW_BLOCKS], bias_cols[:, ROW_BLOCKS : 2 * ROW_BLOCKS])
+        nc.vector.tensor_add(bias[:], bias_t[:, 0:ROW_BLOCKS], bias_t[:, ROW_BLOCKS : 2 * ROW_BLOCKS])
 
-        for b in range(BLOCKS):
-            gate = []
-            for g in range(GATES):
-                m = g * BLOCKS + b
-                acc = psum.tile([P, N], F32, name="acc")
-                for k in range(K_TILES):
-                    nc.tensor.matmul(
-                        acc[:], weights[k][:, m * P : (m + 1) * P], acts[k][:], start=(k == 0), stop=(k == K_TILES - 1)
-                    )
-                squashed = work.tile([P, N], F32, name=f"gate{g}")
-                nc.scalar.activation(squashed[:], acc[:], TANH if g == GATE_U else SIGMOID, bias=bias[:, m : m + 1])
-                gate.append(squashed)
+        def multiply(acc, b, g, k):
+            w = w_half[b // PAIR][k]
+            first = (b % PAIR) * P
+            nc.tensor.matmul(acc[:], w[:, g, first : first + P], acts[k][:], start=(k == 0), stop=(k == K_TILES - 1))
 
+        def squash(acc, b, g):
+            m = g * BLOCKS + b
+            squashed = work.tile([P, N], F32, name=f"gate{g}")
+            nc.scalar.activation(squashed[:], acc[:], TANH if g == GATE_U else SIGMOID, bias=bias[:, m : m + 1])
+            return squashed
+
+        def finish(b, gate):
             kept = work.tile([P, N], F32, name="kept")
             nc.vector.tensor_mul(kept[:], gate[GATE_F][:], cells[b][:])
             fresh = work.tile([P, N], F32, name="fresh")
@@ -81,6 +82,22 @@ def tile_pgndecoder_s_kernel(tc, base, x, h0, c0, W_ih, W_hh, b_ih, b_hh, offs, 
             nc.vector.tensor_add(cnew[:], kept[:], fresh[:])
             tanh_c = work.tile([P, N], F32, name="tanh_c")
             nc.scalar.activation(tanh_c[:], cnew[:], TANH)
-
             nc.vector.tensor_tensor(windows[b][:].indirect(offsets[:]), gate[GATE_O][:], tanh_c[:], MULT)
             nc.sync.dma_start(out[b * P : (b + 1) * P, :], windows[b][:])
+
+        banks = [[psum.tile([P, N], F32, name="acc") for g in range(GATES)] for b in range(PAIR)]
+        for k in range(K_TILES):
+            for b in range(PAIR):
+                for g in range(GATES):
+                    multiply(banks[b][g], b, g, k)
+        for b in range(PAIR):
+            finish(b, [squash(banks[b][g], b, g) for g in range(GATES)])
+
+        for b in range(PAIR, BLOCKS):
+            gate = []
+            for g in range(GATES):
+                acc = psum.tile([P, N], F32, name="acc")
+                for k in range(K_TILES):
+                    multiply(acc, b, g, k)
+                gate.append(squash(acc, b, g))
+            finish(b, gate)

@@ -13,6 +13,7 @@ BLOCKS = H // P
 ROW_BLOCKS = GATES * BLOCKS
 GATE_I, GATE_F, GATE_U, GATE_O = 0, 1, 2, 3
 PAIR = 2
+BANKS = 8
 SQ = 32
 
 FLOPS = 2 * (IN + H) * GATES * H * N
@@ -23,10 +24,18 @@ def tile_pgndecoder_s_kernel(tc, base, x, h0, c0, W_ih, W_hh, b_ih, b_hh, offs, 
     with (
         tc.tile_pool(name="held", bufs=1) as held,
         tc.tile_pool(name="work", bufs=2) as work,
-        tc.psum_pool(name="psum", bufs=GATES * PAIR) as psum,
+        tc.psum_pool(name="psum", bufs=BANKS) as psum,
     ):
-        offsets = held.tile([P, N // 16], U16, name="offsets")
-        nc.sync.dma_start(offsets[:], offs)
+        bias_in = held.tile([P, SQ], F32, name="bias_in", align_bytes=64)
+        for a in range(P // SQ):
+            for v, b_dram in enumerate((b_ih, b_hh)):
+                first = a * SQ + v * ROW_BLOCKS
+                runs = b_dram.rearrange("(m a i) o -> a m (i o)", a=P // SQ, i=SQ)
+                nc.gpsimd.dma_start(bias_in[first : first + ROW_BLOCKS, :], runs[a])
+        bias_t = held.tile([P, SQ], F32, name="bias_t", align_bytes=64)
+        nc.vector.transpose(bias_t[:], bias_in[:])
+        bias = held.tile([P, ROW_BLOCKS], F32, name="bias")
+        nc.vector.tensor_add(bias[:], bias_t[:, 0:ROW_BLOCKS], bias_t[:, ROW_BLOCKS : 2 * ROW_BLOCKS])
 
         sources = [(x, W_ih, t) for t in range(K_TILES_X)] + [(h0, W_hh, t) for t in range(K_TILES_H)]
         acts = []
@@ -34,70 +43,84 @@ def tile_pgndecoder_s_kernel(tc, base, x, h0, c0, W_ih, W_hh, b_ih, b_hh, offs, 
             act = held.tile([P, N], BF16, name=f"act{k}")
             nc.scalar.dma_start(act[:], act_dram[t * P : (t + 1) * P, :])
             acts.append(act)
-        w_half = [[], []]
-        for half in range(2):
+
+        def load_weights(half):
+            tiles = []
             for k, (act_dram, w_dram, t) in enumerate(sources):
                 w = held.tile([P, GATES, PAIR * P], BF16, name=f"w{half}_{k}")
                 by_gate = w_dram[t * P : (t + 1) * P, :].rearrange("p (g c) -> p g c", g=GATES)
                 nc.sync.dma_start(w[:], by_gate[:, :, half * PAIR * P : (half + 1) * PAIR * P])
-                w_half[half].append(w)
+                tiles.append(w)
+            return tiles
 
-        cells, windows = [], []
-        for b in range(BLOCKS):
+        def load_cell_and_window(b):
             cell = held.tile([P, N], F32, name=f"cell{b}")
             nc.sync.dma_start(cell[:], c0[b * P : (b + 1) * P, :])
-            cells.append(cell)
             window = held.tile([P, SLOTS], F32, name=f"window{b}")
             nc.sync.dma_start(window[:], base[b * P : (b + 1) * P, :])
-            windows.append(window)
+            return cell, window
 
-        bias_in = held.tile([P, SQ], F32, name="bias_in", align_bytes=64)
-        for a in range(P // SQ):
-            for v, b_dram in enumerate((b_ih, b_hh)):
-                first = a * SQ + v * ROW_BLOCKS
-                runs = b_dram.rearrange("(m a i) o -> a m (i o)", a=P // SQ, i=SQ)
-                nc.scalar.dma_start(bias_in[first : first + ROW_BLOCKS, :], runs[a])
-        bias_t = held.tile([P, SQ], F32, name="bias_t", align_bytes=64)
-        nc.vector.transpose(bias_t[:], bias_in[:])
-        bias = held.tile([P, ROW_BLOCKS], F32, name="bias")
-        nc.vector.tensor_add(bias[:], bias_t[:, 0:ROW_BLOCKS], bias_t[:, ROW_BLOCKS : 2 * ROW_BLOCKS])
+        w_first = load_weights(0)
+        offsets = held.tile([P, N // 16], U16, name="offsets")
+        nc.sync.dma_start(offsets[:], offs)
+        first_pair = [load_cell_and_window(b) for b in range(PAIR)]
+        w_half = [w_first, load_weights(1)]
+        cells_and_windows = first_pair + [load_cell_and_window(b) for b in range(PAIR, BLOCKS)]
+        cells = [cell for cell, window in cells_and_windows]
+        windows = [window for cell, window in cells_and_windows]
 
-        def multiply(acc, b, g, k):
-            w = w_half[b // PAIR][k]
-            first = (b % PAIR) * P
-            nc.tensor.matmul(acc[:], w[:, g, first : first + P], acts[k][:], start=(k == 0), stop=(k == K_TILES - 1))
+
+        def multiply(acc, b, g, k, seqs):
+            w = w_half[b // PAIR][k][:, g, (b % PAIR) * P : (b % PAIR + 1) * P]
+            first, count = seqs
+            nc.tensor.matmul(acc[:], w, acts[k][:, first : first + count], start=(k == 0), stop=(k == K_TILES - 1))
 
         def squash(acc, b, g):
             m = g * BLOCKS + b
-            squashed = work.tile([P, N], F32, name=f"gate{g}")
+            squashed = work.tile(acc.shape, F32, name=f"gate{g}")
             nc.scalar.activation(squashed[:], acc[:], TANH if g == GATE_U else SIGMOID, bias=bias[:, m : m + 1])
             return squashed
 
-        def finish(b, gate):
-            kept = work.tile([P, N], F32, name="kept")
-            nc.vector.tensor_mul(kept[:], gate[GATE_F][:], cells[b][:])
-            fresh = work.tile([P, N], F32, name="fresh")
-            nc.vector.tensor_mul(fresh[:], gate[GATE_I][:], gate[GATE_U][:])
-            cnew = work.tile([P, N], F32, name="cnew")
+        def tanh_of_new_cell(b, gate_i, gate_f, gate_u, seqs):
+            first, count = seqs
+            kept = work.tile(gate_f.shape, F32, name="kept")
+            nc.vector.tensor_mul(kept[:], gate_f[:], cells[b][:, first : first + count])
+            fresh = work.tile(gate_f.shape, F32, name="fresh")
+            nc.vector.tensor_mul(fresh[:], gate_i[:], gate_u[:])
+            cnew = work.tile(gate_f.shape, F32, name="cnew")
             nc.vector.tensor_add(cnew[:], kept[:], fresh[:])
-            tanh_c = work.tile([P, N], F32, name="tanh_c")
+            tanh_c = work.tile(gate_f.shape, F32, name="tanh_c")
             nc.scalar.activation(tanh_c[:], cnew[:], TANH)
-            nc.vector.tensor_tensor(windows[b][:].indirect(offsets[:]), gate[GATE_O][:], tanh_c[:], MULT)
+            return tanh_c
+
+        def place(b, gate_o, tanh_c, seqs):
+            first, count = seqs
+            listed = offsets[:, first // 16 : (first + count) // 16]
+            nc.vector.tensor_tensor(windows[b][:].indirect(listed), gate_o[:], tanh_c[:], MULT)
+
+        def store(b):
             nc.sync.dma_start(out[b * P : (b + 1) * P, :], windows[b][:])
 
-        banks = [[psum.tile([P, N], F32, name="acc") for g in range(GATES)] for b in range(PAIR)]
+        everyone = (0, N)
+        banks = [psum.tile([P, N], F32, name="acc") for g in range(GATES)]
         for k in range(K_TILES):
-            for b in range(PAIR):
-                for g in range(GATES):
-                    multiply(banks[b][g], b, g, k)
-        for b in range(PAIR):
-            finish(b, [squash(banks[b][g], b, g) for g in range(GATES)])
-
-        for b in range(PAIR, BLOCKS):
-            gate = []
             for g in range(GATES):
-                acc = psum.tile([P, N], F32, name="acc")
+                multiply(banks[g], 0, g, k, everyone)
+        gate = [squash(banks[g], 0, g) for g in range(GATES)]
+        tanh_c = tanh_of_new_cell(0, gate[GATE_I], gate[GATE_F], gate[GATE_U], everyone)
+        place(0, gate[GATE_O], tanh_c, everyone)
+        store(0)
+
+        pieces = [(b, everyone) for b in range(1, BLOCKS - 1)] + [(BLOCKS - 1, (0, N // 2)), (BLOCKS - 1, (N // 2, N // 2))]
+        for b, seqs in pieces:
+            gate = {}
+            for g in (GATE_I, GATE_F, GATE_U, GATE_O):
+                acc = psum.tile([P, seqs[1]], F32, name="acc")
                 for k in range(K_TILES):
-                    multiply(acc, b, g, k)
-                gate.append(squash(acc, b, g))
-            finish(b, gate)
+                    multiply(acc, b, g, k, seqs)
+                if g == GATE_O:
+                    tanh_c = tanh_of_new_cell(b, gate[GATE_I], gate[GATE_F], gate[GATE_U], seqs)
+                gate[g] = squash(acc, b, g)
+            place(b, gate[GATE_O], tanh_c, seqs)
+            if sum(seqs) == N:
+                store(b)

@@ -14,6 +14,7 @@ ROW_BLOCKS = GATES * BLOCKS
 GATE_I, GATE_F, GATE_U, GATE_O = 0, 1, 2, 3
 PAIR = 2
 BANKS = 8
+WARM_UP = 5
 SQ = 32
 
 FLOPS = 2 * (IN + H) * GATES * H * N
@@ -26,6 +27,12 @@ def tile_pgndecoder_s_kernel(tc, base, x, h0, c0, W_ih, W_hh, b_ih, b_hh, offs, 
         tc.tile_pool(name="work", bufs=2) as work,
         tc.psum_pool(name="psum", bufs=BANKS) as psum,
     ):
+        zeros = held.tile([P, N], BF16, name="zeros")
+        nc.vector.memset(zeros[:], 0.0)
+        unread = psum.tile([P, N], F32, name="unread", tag="acc")
+        for i in range(WARM_UP):
+            nc.tensor.matmul(unread[:], zeros[:, 0:P], zeros[:], start=True, stop=True)
+
         bias_in = held.tile([P, SQ], F32, name="bias_in", align_bytes=64)
         for a in range(P // SQ):
             for v, b_dram in enumerate((b_ih, b_hh)):

@@ -14,7 +14,7 @@ ROW_BLOCKS = GATES * BLOCKS
 GATE_I, GATE_F, GATE_U, GATE_O = 0, 1, 2, 3
 PAIR = 2
 BANKS = 8
-WARM_UP = 5
+WARM_UP = 3
 SQ = 32
 
 FLOPS = 2 * (IN + H) * GATES * H * N
@@ -118,7 +118,8 @@ def tile_pgndecoder_s_kernel(tc, base, x, h0, c0, W_ih, W_hh, b_ih, b_hh, offs, 
         place(0, gate[GATE_O], tanh_c, everyone)
         store(0)
 
-        pieces = [(b, everyone) for b in range(1, BLOCKS - 1)] + [(BLOCKS - 1, (0, N // 2)), (BLOCKS - 1, (N // 2, N // 2))]
+        cut = 5 * N // 8
+        pieces = [(b, everyone) for b in range(1, BLOCKS - 1)] + [(BLOCKS - 1, (0, cut)), (BLOCKS - 1, (cut, N - cut))]
         for b, seqs in pieces:
             gate = {}
             for g in (GATE_I, GATE_F, GATE_U, GATE_O):

@@ -12,6 +12,7 @@ K_TILES = K_TILES_X + K_TILES_H
 BLOCKS = H // P
 ROW_BLOCKS = GATES * BLOCKS
 GATE_I, GATE_F, GATE_U, GATE_O = 0, 1, 2, 3
+FIRST_GATES, LATER_GATES = (GATE_I, GATE_F), (GATE_U, GATE_O)
 PAIR = 2
 BANKS = 8
 WARM_UP = 3
@@ -51,14 +52,17 @@ def tile_pgndecoder_s_kernel(tc, base, x, h0, c0, W_ih, W_hh, b_ih, b_hh, offs, 
             nc.scalar.dma_start(act[:], act_dram[t * P : (t + 1) * P, :])
             acts.append(act)
 
-        def load_weights(half):
+        weights = {}
+
+        def load_weights(pair, gates):
             tiles = []
             for k, (act_dram, w_dram, t) in enumerate(sources):
-                w = held.tile([P, GATES, PAIR * P], BF16, name=f"w{half}_{k}")
+                w = held.tile([P, len(gates), PAIR * P], BF16, name=f"w{pair}_{gates[0]}_{k}")
                 by_gate = w_dram[t * P : (t + 1) * P, :].rearrange("p (g c) -> p g c", g=GATES)
-                nc.sync.dma_start(w[:], by_gate[:, :, half * PAIR * P : (half + 1) * PAIR * P])
+                nc.sync.dma_start(w[:], by_gate[:, gates[0] : gates[-1] + 1, pair * PAIR * P : (pair + 1) * PAIR * P])
                 tiles.append(w)
-            return tiles
+            for i, g in enumerate(gates):
+                weights[pair, g] = (tiles, i)
 
         def load_cell_and_window(b):
             cell = held.tile([P, N], F32, name=f"cell{b}")
@@ -67,18 +71,20 @@ def tile_pgndecoder_s_kernel(tc, base, x, h0, c0, W_ih, W_hh, b_ih, b_hh, offs, 
             nc.sync.dma_start(window[:], base[b * P : (b + 1) * P, :])
             return cell, window
 
-        w_first = load_weights(0)
+        load_weights(0, FIRST_GATES)
+        load_weights(0, LATER_GATES)
         offsets = held.tile([P, N // 16], U16, name="offsets")
         nc.sync.dma_start(offsets[:], offs)
         first_pair = [load_cell_and_window(b) for b in range(PAIR)]
-        w_half = [w_first, load_weights(1)]
+        load_weights(1, FIRST_GATES + LATER_GATES)
         cells_and_windows = first_pair + [load_cell_and_window(b) for b in range(PAIR, BLOCKS)]
         cells = [cell for cell, window in cells_and_windows]
         windows = [window for cell, window in cells_and_windows]
 
 
         def multiply(acc, b, g, k, seqs):
-            w = w_half[b // PAIR][k][:, g, (b % PAIR) * P : (b % PAIR + 1) * P]
+            tiles, place_in_tile = weights[b // PAIR, g]
+            w = tiles[k][:, place_in_tile, (b % PAIR) * P : (b % PAIR + 1) * P]
             first, count = seqs
             nc.tensor.matmul(acc[:], w, acts[k][:, first : first + count], start=(k == 0), stop=(k == K_TILES - 1))
 
@@ -109,20 +115,20 @@ def tile_pgndecoder_s_kernel(tc, base, x, h0, c0, W_ih, W_hh, b_ih, b_hh, offs, 
             nc.sync.dma_start(out[b * P : (b + 1) * P, :], windows[b][:])
 
         everyone = (0, N)
-        banks = [psum.tile([P, N], F32, name="acc") for g in range(GATES)]
+        early = [(b, g) for b in range(PAIR) for g in FIRST_GATES]
+        banks = {bg: psum.tile([P, N], F32, name="acc") for bg in early}
         for k in range(K_TILES):
-            for g in range(GATES):
-                multiply(banks[g], 0, g, k, everyone)
-        gate = [squash(banks[g], 0, g) for g in range(GATES)]
-        tanh_c = tanh_of_new_cell(0, gate[GATE_I], gate[GATE_F], gate[GATE_U], everyone)
-        place(0, gate[GATE_O], tanh_c, everyone)
-        store(0)
+            for b, g in early:
+                multiply(banks[b, g], b, g, k, everyone)
+        early_gate = {(b, g): squash(banks[b, g], b, g) for b, g in early}
 
         cut = 5 * N // 8
-        pieces = [(b, everyone) for b in range(1, BLOCKS - 1)] + [(BLOCKS - 1, (0, cut)), (BLOCKS - 1, (cut, N - cut))]
+        pieces = [(b, everyone) for b in range(BLOCKS - 1)] + [(BLOCKS - 1, (0, cut)), (BLOCKS - 1, (cut, N - cut))]
         for b, seqs in pieces:
-            gate = {}
+            gate = {g: early_gate[b, g] for g in FIRST_GATES if (b, g) in early_gate}
             for g in (GATE_I, GATE_F, GATE_U, GATE_O):
+                if g in gate:
+                    continue
                 acc = psum.tile([P, seqs[1]], F32, name="acc")
                 for k in range(K_TILES):
                     multiply(acc, b, g, k, seqs)

@@ -64,22 +64,28 @@ def tile_pgndecoder_s_kernel(tc, base, x, h0, c0, W_ih, W_hh, b_ih, b_hh, offs, 
             for i, g in enumerate(gates):
                 weights[pair, g] = (tiles, i)
 
-        def load_cell_and_window(b):
-            cell = held.tile([P, N], F32, name=f"cell{b}")
-            nc.sync.dma_start(cell[:], c0[b * P : (b + 1) * P, :])
+        def load_cells(first, count):
+            tile = held.tile([P, count, N], F32, name=f"cells{first}")
+            nc.sync.dma_start(tile[:], c0[first * P : (first + count) * P, :].rearrange("(b p) n -> p b n", p=P))
+            return [tile[:, i, :] for i in range(count)]
+
+        def load_window(b):
             window = held.tile([P, SLOTS], F32, name=f"window{b}")
             nc.sync.dma_start(window[:], base[b * P : (b + 1) * P, :])
-            return cell, window
+            return window
 
         load_weights(0, FIRST_GATES)
         load_weights(0, LATER_GATES)
         offsets = held.tile([P, N // 16], U16, name="offsets")
         nc.sync.dma_start(offsets[:], offs)
-        first_pair = [load_cell_and_window(b) for b in range(PAIR)]
+        cells, windows = [], []
+        for b in range(PAIR):
+            cells.extend(load_cells(b, 1))
+            windows.append(load_window(b))
         load_weights(1, FIRST_GATES + LATER_GATES)
-        cells_and_windows = first_pair + [load_cell_and_window(b) for b in range(PAIR, BLOCKS)]
-        cells = [cell for cell, window in cells_and_windows]
-        windows = [window for cell, window in cells_and_windows]
+        cells.extend(load_cells(PAIR, PAIR))
+        for b in range(PAIR, BLOCKS):
+            windows.append(load_window(b))
 
 
         def multiply(acc, b, g, k, seqs):

@@ -47,16 +47,20 @@ def tile_pgndecoder_s_kernel(tc, base, x, h0, c0, W_ih, W_hh, b_ih, b_hh, offs, 
 
         sources = [(x, W_ih, t) for t in range(K_TILES_X)] + [(h0, W_hh, t) for t in range(K_TILES_H)]
         acts = []
-        for k, (act_dram, w_dram, t) in enumerate(sources):
+
+        def load_moving(k):
+            act_dram, w_dram, t = sources[k]
             act = held.tile([P, N], BF16, name=f"act{k}")
-            nc.scalar.dma_start(act[:], act_dram[t * P : (t + 1) * P, :])
+            nc.sync.dma_start(act[:], act_dram[t * P : (t + 1) * P, :])
             acts.append(act)
 
         weights = {}
 
-        def load_weights(pair, gates):
+        def load_weights(pair, gates, with_moving=False):
             tiles = []
             for k, (act_dram, w_dram, t) in enumerate(sources):
+                if with_moving:
+                    load_moving(k)
                 w = held.tile([P, len(gates), PAIR * P], BF16, name=f"w{pair}_{gates[0]}_{k}")
                 by_gate = w_dram[t * P : (t + 1) * P, :].rearrange("p (g c) -> p g c", g=GATES)
                 nc.sync.dma_start(w[:], by_gate[:, gates[0] : gates[-1] + 1, pair * PAIR * P : (pair + 1) * PAIR * P])
@@ -74,7 +78,7 @@ def tile_pgndecoder_s_kernel(tc, base, x, h0, c0, W_ih, W_hh, b_ih, b_hh, offs, 
             nc.sync.dma_start(window[:], base[b * P : (b + 1) * P, :])
             return window
 
-        load_weights(0, FIRST_GATES)
+        load_weights(0, FIRST_GATES, with_moving=True)
         load_weights(0, LATER_GATES)
         offsets = held.tile([P, N // 16], U16, name="offsets")
         nc.sync.dma_start(offsets[:], offs)

@@ -54,6 +54,9 @@ def tile_pgndecoder_s_kernel(tc, base, x, h0, c0, W_ih, W_hh, b_ih, b_hh, offs, 
             nc.sync.dma_start(act[:], act_dram[t * P : (t + 1) * P, :])
             acts.append(act)
 
+        unused = held.tile([P, 1], F32, name="unused")
+        nc.scalar.activation(unused[:], zeros[:, 0:1], SIGMOID)
+
         weights = {}
 
         def load_weights(pair, gates, with_moving=False):

@@ -66,7 +66,12 @@ def tile_pgndecoder_s_kernel(tc, base, x, h0, c0, W_ih, W_hh, b_ih, b_hh, offs, 
                     load_moving(k)
                 w = held.tile([P, len(gates), PAIR * P], BF16, name=f"w{pair}_{gates[0]}_{k}")
                 by_gate = w_dram[t * P : (t + 1) * P, :].rearrange("p (g c) -> p g c", g=GATES)
-                nc.sync.dma_start(w[:], by_gate[:, gates[0] : gates[-1] + 1, pair * PAIR * P : (pair + 1) * PAIR * P])
+                columns = slice(pair * PAIR * P, (pair + 1) * PAIR * P)
+                if with_moving and k == 0:
+                    for i, g in enumerate(gates):
+                        nc.sync.dma_start(w[:, i, :], by_gate[:, g, columns])
+                else:
+                    nc.sync.dma_start(w[:], by_gate[:, gates[0] : gates[-1] + 1, columns])
                 tiles.append(w)
             for i, g in enumerate(gates):
                 weights[pair, g] = (tiles, i)
@@ -86,8 +91,8 @@ def tile_pgndecoder_s_kernel(tc, base, x, h0, c0, W_ih, W_hh, b_ih, b_hh, offs, 
         offsets = held.tile([P, N // 16], U16, name="offsets")
         nc.sync.dma_start(offsets[:], offs)
         cells, windows = [], []
+        cells.extend(load_cells(0, PAIR))
         for b in range(PAIR):
-            cells.extend(load_cells(b, 1))
             windows.append(load_window(b))
         load_weights(1, FIRST_GATES + LATER_GATES)
         cells.extend(load_cells(PAIR, PAIR))
@@ -128,7 +133,7 @@ def tile_pgndecoder_s_kernel(tc, base, x, h0, c0, W_ih, W_hh, b_ih, b_hh, offs, 
             nc.sync.dma_start(out[b * P : (b + 1) * P, :], windows[b][:])
 
         everyone = (0, N)
-        early = [(b, g) for b in range(PAIR) for g in FIRST_GATES]
+        early = [(b, g) for g in FIRST_GATES for b in range(PAIR)]
         banks = {bg: psum.tile([P, N], F32, name="acc") for bg in early}
         for k in range(K_TILES):
             for b, g in early:

import concourse.mybir as mybir

BF16, F32, U16 = mybir.dt.bfloat16, mybir.dt.float32, mybir.dt.uint16
SIGMOID = mybir.ActivationFunctionType.Sigmoid
TANH = mybir.ActivationFunctionType.Tanh
MULT = mybir.AluOpType.mult

P = 128
IN, H, GATES, SLOTS, N = 640, 512, 4, 1024, 512
K_TILES_X, K_TILES_H = IN // P, H // P
K_TILES = K_TILES_X + K_TILES_H
BLOCKS = H // P
ROW_BLOCKS = GATES * BLOCKS
GATE_I, GATE_F, GATE_U, GATE_O = 0, 1, 2, 3
FIRST_GATES, LATER_GATES = (GATE_I, GATE_F), (GATE_U, GATE_O)
PAIR = 2
BANKS = 8
WARM_UP = 3
SQ = 32

FLOPS = 2 * (IN + H) * GATES * H * N


def tile_pgndecoder_s_kernel(tc, base, x, h0, c0, W_ih, W_hh, b_ih, b_hh, offs, out):
    nc = tc.nc
    with (
        tc.tile_pool(name="held", bufs=1) as held,
        tc.tile_pool(name="work", bufs=2) as work,
        tc.psum_pool(name="psum", bufs=BANKS) as psum,
    ):
        zeros = held.tile([P, N], BF16, name="zeros")
        nc.vector.memset(zeros[:], 0.0)
        unread = psum.tile([P, N], F32, name="unread", tag="acc")
        for i in range(WARM_UP):
            nc.tensor.matmul(unread[:], zeros[:, 0:P], zeros[:], start=True, stop=True)

        bias_in = held.tile([P, SQ], F32, name="bias_in", align_bytes=64)
        for a in range(P // SQ):
            for v, b_dram in enumerate((b_ih, b_hh)):
                first = a * SQ + v * ROW_BLOCKS
                runs = b_dram.rearrange("(m a i) o -> a m (i o)", a=P // SQ, i=SQ)
                nc.gpsimd.dma_start(bias_in[first : first + ROW_BLOCKS, :], runs[a])
        bias_t = held.tile([P, SQ], F32, name="bias_t", align_bytes=64)
        nc.vector.transpose(bias_t[:], bias_in[:])
        bias = held.tile([P, ROW_BLOCKS], F32, name="bias")
        nc.vector.tensor_add(bias[:], bias_t[:, 0:ROW_BLOCKS], bias_t[:, ROW_BLOCKS : 2 * ROW_BLOCKS])

        sources = [(x, W_ih, t) for t in range(K_TILES_X)] + [(h0, W_hh, t) for t in range(K_TILES_H)]
        acts = []

        def load_moving(k):
            act_dram, w_dram, t = sources[k]
            act = held.tile([P, N], BF16, name=f"act{k}")
            nc.sync.dma_start(act[:], act_dram[t * P : (t + 1) * P, :])
            acts.append(act)

        unused = held.tile([P, 1], F32, name="unused")
        nc.scalar.activation(unused[:], zeros[:, 0:1], SIGMOID)

        weights = {}

        def load_weights(pair, gates, with_moving=False):
            tiles = []
            for k, (act_dram, w_dram, t) in enumerate(sources):
                if with_moving:
                    load_moving(k)
                w = held.tile([P, len(gates), PAIR * P], BF16, name=f"w{pair}_{gates[0]}_{k}")
                by_gate = w_dram[t * P : (t + 1) * P, :].rearrange("p (g c) -> p g c", g=GATES)
                columns = slice(pair * PAIR * P, (pair + 1) * PAIR * P)
                if with_moving and k == 0:
                    for i, g in enumerate(gates):
                        nc.sync.dma_start(w[:, i, :], by_gate[:, g, columns])
                else:
                    nc.sync.dma_start(w[:], by_gate[:, gates[0] : gates[-1] + 1, columns])
                tiles.append(w)
            for i, g in enumerate(gates):
                weights[pair, g] = (tiles, i)

        def load_cells(first, count):
            tile = held.tile([P, count, N], F32, name=f"cells{first}")
            nc.sync.dma_start(tile[:], c0[first * P : (first + count) * P, :].rearrange("(b p) n -> p b n", p=P))
            return [tile[:, i, :] for i in range(count)]

        def load_window(b):
            window = held.tile([P, SLOTS], F32, name=f"window{b}")
            nc.sync.dma_start(window[:], base[b * P : (b + 1) * P, :])
            return window

        load_weights(0, FIRST_GATES, with_moving=True)
        load_weights(0, LATER_GATES)
        offsets = held.tile([P, N // 16], U16, name="offsets")
        nc.sync.dma_start(offsets[:], offs)
        cells, windows = [], []
        cells.extend(load_cells(0, PAIR))
        for b in range(PAIR):
            windows.append(load_window(b))
        load_weights(1, FIRST_GATES + LATER_GATES)
        cells.extend(load_cells(PAIR, PAIR))
        for b in range(PAIR, BLOCKS):
            windows.append(load_window(b))


        def multiply(acc, b, g, k, seqs):
            tiles, place_in_tile = weights[b // PAIR, g]
            w = tiles[k][:, place_in_tile, (b % PAIR) * P : (b % PAIR + 1) * P]
            first, count = seqs
            nc.tensor.matmul(acc[:], w, acts[k][:, first : first + count], start=(k == 0), stop=(k == K_TILES - 1))

        def squash(acc, b, g):
            m = g * BLOCKS + b
            squashed = work.tile(acc.shape, F32, name=f"gate{g}")
            nc.scalar.activation(squashed[:], acc[:], TANH if g == GATE_U else SIGMOID, bias=bias[:, m : m + 1])
            return squashed

        def tanh_of_new_cell(b, gate_i, gate_f, gate_u, seqs):
            first, count = seqs
            kept = work.tile(gate_f.shape, F32, name="kept")
            nc.vector.tensor_mul(kept[:], gate_f[:], cells[b][:, first : first + count])
            fresh = work.tile(gate_f.shape, F32, name="fresh")
            nc.vector.tensor_mul(fresh[:], gate_i[:], gate_u[:])
            cnew = work.tile(gate_f.shape, F32, name="cnew")
            nc.vector.tensor_add(cnew[:], kept[:], fresh[:])
            tanh_c = work.tile(gate_f.shape, F32, name="tanh_c")
            nc.scalar.activation(tanh_c[:], cnew[:], TANH)
            return tanh_c

        def place(b, gate_o, tanh_c, seqs):
            first, count = seqs
            listed = offsets[:, first // 16 : (first + count) // 16]
            nc.vector.tensor_tensor(windows[b][:].indirect(listed), gate_o[:], tanh_c[:], MULT)

        def store(b):
            nc.sync.dma_start(out[b * P : (b + 1) * P, :], windows[b][:])

        everyone = (0, N)
        early = [(b, g) for g in FIRST_GATES for b in range(PAIR)]
        banks = {bg: psum.tile([P, N], F32, name="acc") for bg in early}
        for k in range(K_TILES):
            for b, g in early:
                multiply(banks[b, g], b, g, k, everyone)
        early_gate = {(b, g): squash(banks[b, g], b, g) for b, g in early}

        cut = 5 * N // 8
        pieces = [(b, everyone) for b in range(BLOCKS - 1)] + [(BLOCKS - 1, (0, cut)), (BLOCKS - 1, (cut, N - cut))]
        for b, seqs in pieces:
            gate = {g: early_gate[b, g] for g in FIRST_GATES if (b, g) in early_gate}
            for g in (GATE_I, GATE_F, GATE_U, GATE_O):
                if g in gate:
                    continue
                acc = psum.tile([P, seqs[1]], F32, name="acc")
                for k in range(K_TILES):
                    multiply(acc, b, g, k, seqs)
                if g == GATE_O:
                    tanh_c = tanh_of_new_cell(b, gate[GATE_I], gate[GATE_F], gate[GATE_U], seqs)
                gate[g] = squash(acc, b, g)
            place(b, gate[GATE_O], tanh_c, seqs)
            if sum(seqs) == N:
                store(b)
